import numpy as np
import ml_dtypes

BF16 = ml_dtypes.bfloat16


def bf(x):
    return np.asarray(x, np.float32).astype(BF16)


def f32(x):
    return np.asarray(x, np.float32)


def f64(x):
    return np.asarray(x).astype(np.float64)


def striped(idx):
    return np.tile(idx.reshape(-1, 16).T, (8, 1))


V, D, DQ, M, N, HD, HALF = 1024, 128, 128, 256, 256, 64, 32
BASE = 10000.0


def rope_tables():
    inv = np.float32(1.0) / (np.float32(BASE) ** (np.arange(HALF, dtype=np.float32) / np.float32(HALF)))
    ang = inv[:, None] * np.arange(N, dtype=np.float32)[None, :]
    ang = np.tile(ang, (DQ // HALF, 1))
    return f32(np.cos(f64(ang))), f32(np.sin(f64(ang)))


def setup_inputs():
    cosr, sinr = rope_tables()
    return {"table": bf(np.random.standard_normal((D, V))), "w": bf(np.random.standard_normal((D, M)) / np.sqrt(D)), "b": f32(0.1 * np.random.standard_normal((M, 1))), "cosr": cosr, "sinr": sinr, "offs": striped(np.random.permutation(np.tile(np.arange(V), 2))[:N])}


def reference(table, w, b, cosr, sinr, offs):
    idx = offs[:16].T.reshape(-1)
    p = f64(w).T @ f64(table)[:, idx] + f64(b)
    q = p[:DQ]
    q4 = q.reshape(DQ // HD, HD // HALF, HALF, N)
    r = np.stack([-q4[:, 1], q4[:, 0]], axis=1).reshape(DQ, N)
    return np.concatenate([q * f64(cosr) + r * f64(sinr), p[DQ:]], axis=0)

@@ -1,0 +1,61 @@
+import concourse.mybir as mybir
+
+P = 128
+V = 1024
+N = 256
+HEAD = 64
+HALF = 32
+FLOPS = 2 * P * 2 * P * N
+
+BF16, F32, U16 = mybir.dt.bfloat16, mybir.dt.float32, mybir.dt.uint16
+ADD, MULT = mybir.AluOpType.add, mybir.AluOpType.mult
+IDENTITY = mybir.ActivationFunctionType.Identity
+
+
+def tile_kelso_model_kernel(tc, table, w, b, cosr, sinr, offs, out):
+    nc = tc.nc
+    with tc.tile_pool(name="held", bufs=1) as held, tc.psum_pool(name="banks", bufs=1) as banks:
+        offsets = held.tile([P, N // 16], U16, name="offsets")
+        nc.sync.dma_start(offsets[:], offs)
+        table_sb = held.tile([P, V], BF16, name="table_sb")
+        nc.sync.dma_start(table_sb[:], table)
+        w_sb = held.tile([P, 2 * P], BF16, name="w_sb")
+        nc.scalar.dma_start(w_sb[:], w)
+        cos_sb = held.tile([P, N], F32, name="cos_sb")
+        nc.scalar.dma_start(cos_sb[:], cosr)
+        sin_sb = held.tile([P, N], F32, name="sin_sb")
+        nc.scalar.dma_start(sin_sb[:], sinr)
+        b_qk = held.tile([P, 1], F32, name="b_qk")
+        nc.gpsimd.dma_start(b_qk[:], b[0:P, :])
+        b_val = held.tile([P, 1], F32, name="b_val")
+        nc.gpsimd.dma_start(b_val[:], b[P : 2 * P, :])
+
+        w_rot = held.tile([P, P], BF16, name="w_rot")
+        b_rot = held.tile([P, 1], F32, name="b_rot")
+        for low in range(0, P, HEAD):
+            high = low + HALF
+            nc.gpsimd.dma_start(b_rot[low : low + HALF, :], b[high : high + HALF, :])
+            nc.gpsimd.dma_start(b_rot[high : high + HALF, :], b[low : low + HALF, :])
+            nc.vector.tensor_scalar_mul(b_rot[low : low + HALF, :], b_rot[low : low + HALF, :], -1.0)
+            nc.vector.tensor_scalar_mul(w_rot[:, low : low + HALF], w_sb[:, high : high + HALF], -1.0)
+            nc.vector.tensor_copy(w_rot[:, high : high + HALF], w_sb[:, low : low + HALF])
+
+        picked = table_sb[:].indirect(offsets[:])
+        p_qk = banks.tile([P, N], F32, name="p_qk")
+        nc.tensor.matmul(p_qk[:], w_sb[:, 0:P], picked, start=True, stop=True)
+        r_qk = banks.tile([P, N], F32, name="r_qk")
+        nc.tensor.matmul(r_qk[:], w_rot[:], picked, start=True, stop=True)
+        p_val = banks.tile([P, N], F32, name="p_val")
+        nc.tensor.matmul(p_val[:], w_sb[:, P : 2 * P], picked, start=True, stop=True)
+
+        with_cos = held.tile([P, N], F32, name="with_cos")
+        nc.vector.scalar_tensor_tensor(with_cos[:], p_qk[:], b_qk[:], cos_sb[:], op0=ADD, op1=MULT)
+        with_sin = held.tile([P, N], F32, name="with_sin")
+        nc.vector.scalar_tensor_tensor(with_sin[:], r_qk[:], b_rot[:], sin_sb[:], op0=ADD, op1=MULT)
+        out_qk = held.tile([P, N], F32, name="out_qk")
+        nc.vector.tensor_add(out_qk[:], with_cos[:], with_sin[:])
+        nc.sync.dma_start(out[0:P, :], out_qk[:])
+
+        out_val = held.tile([P, N], F32, name="out_val")
+        nc.scalar.activation(out_val[:], p_val[:], IDENTITY, bias=b_val[:])
+        nc.scalar.dma_start(out[P : 2 * P, :], out_val[:])

@@ -21,24 +21,25 @@ def tile_kelso_model_kernel(tc, table, w, b, cosr, sinr, offs, out):
         nc.sync.dma_start(table_sb[:], table)
         w_sb = held.tile([P, 2 * P], BF16, name="w_sb")
         nc.scalar.dma_start(w_sb[:], w)
-        cos_sb = held.tile([P, N], F32, name="cos_sb")
-        nc.scalar.dma_start(cos_sb[:], cosr)
-        sin_sb = held.tile([P, N], F32, name="sin_sb")
-        nc.scalar.dma_start(sin_sb[:], sinr)
         b_qk = held.tile([P, 1], F32, name="b_qk")
-        nc.gpsimd.dma_start(b_qk[:], b[0:P, :])
+        nc.sync.dma_start(b_qk[:], b[0:P, :])
         b_val = held.tile([P, 1], F32, name="b_val")
-        nc.gpsimd.dma_start(b_val[:], b[P : 2 * P, :])
+        nc.sync.dma_start(b_val[:], b[P : 2 * P, :])
 
         w_rot = held.tile([P, P], BF16, name="w_rot")
         b_rot = held.tile([P, 1], F32, name="b_rot")
         for low in range(0, P, HEAD):
             high = low + HALF
-            nc.gpsimd.dma_start(b_rot[low : low + HALF, :], b[high : high + HALF, :])
-            nc.gpsimd.dma_start(b_rot[high : high + HALF, :], b[low : low + HALF, :])
+            nc.scalar.dma_start(b_rot[low : low + HALF, :], b[high : high + HALF, :])
+            nc.scalar.dma_start(b_rot[high : high + HALF, :], b[low : low + HALF, :])
             nc.vector.tensor_scalar_mul(b_rot[low : low + HALF, :], b_rot[low : low + HALF, :], -1.0)
             nc.vector.tensor_scalar_mul(w_rot[:, low : low + HALF], w_sb[:, high : high + HALF], -1.0)
             nc.vector.tensor_copy(w_rot[:, high : high + HALF], w_sb[:, low : low + HALF])
+
+        cos_sb = held.tile([P, N], F32, name="cos_sb")
+        nc.scalar.dma_start(cos_sb[:], cosr)
+        sin_sb = held.tile([P, N], F32, name="sin_sb")
+        nc.scalar.dma_start(sin_sb[:], sinr)
 
         picked = table_sb[:].indirect(offsets[:])
         p_qk = banks.tile([P, N], F32, name="p_qk")

@@ -19,12 +19,14 @@ def tile_kelso_model_kernel(tc, table, w, b, cosr, sinr, offs, out):
         nc.sync.dma_start(offsets[:], offs)
         table_sb = held.tile([P, V], BF16, name="table_sb")
         nc.sync.dma_start(table_sb[:], table)
+        cos_sb = held.tile([P, N], F32, name="cos_sb")
+        nc.sync.dma_start(cos_sb[:], cosr)
+        sin_sb = held.tile([P, N], F32, name="sin_sb")
+        nc.sync.dma_start(sin_sb[:], sinr)
         w_sb = held.tile([P, 2 * P], BF16, name="w_sb")
         nc.scalar.dma_start(w_sb[:], w)
         b_qk = held.tile([P, 1], F32, name="b_qk")
-        nc.sync.dma_start(b_qk[:], b[0:P, :])
-        b_val = held.tile([P, 1], F32, name="b_val")
-        nc.sync.dma_start(b_val[:], b[P : 2 * P, :])
+        nc.scalar.dma_start(b_qk[:], b[0:P, :])
 
         w_rot = held.tile([P, P], BF16, name="w_rot")
         b_rot = held.tile([P, 1], F32, name="b_rot")
@@ -36,10 +38,8 @@ def tile_kelso_model_kernel(tc, table, w, b, cosr, sinr, offs, out):
             nc.vector.tensor_scalar_mul(w_rot[:, low : low + HALF], w_sb[:, high : high + HALF], -1.0)
             nc.vector.tensor_copy(w_rot[:, high : high + HALF], w_sb[:, low : low + HALF])
 
-        cos_sb = held.tile([P, N], F32, name="cos_sb")
-        nc.scalar.dma_start(cos_sb[:], cosr)
-        sin_sb = held.tile([P, N], F32, name="sin_sb")
-        nc.scalar.dma_start(sin_sb[:], sinr)
+        b_val = held.tile([P, 1], F32, name="b_val")
+        nc.scalar.dma_start(b_val[:], b[P : 2 * P, :])
 
         picked = table_sb[:].indirect(offsets[:])
         p_qk = banks.tile([P, N], F32, name="p_qk")

@@ -3,7 +3,6 @@ import concourse.mybir as mybir
 P = 128
 V = 1024
 N = 256
-HEAD = 64
 HALF = 32
 FLOPS = 2 * P * 2 * P * N
 
@@ -15,31 +14,39 @@ IDENTITY = mybir.ActivationFunctionType.Identity
 def tile_kelso_model_kernel(tc, table, w, b, cosr, sinr, offs, out):
     nc = tc.nc
     with tc.tile_pool(name="held", bufs=1) as held, tc.psum_pool(name="banks", bufs=1) as banks:
+        b_row = held.tile([1, 2 * P], F32, name="b_row")
+        nc.scalar.dma_start(b_row[:], b.rearrange("m one -> one m"))
         offsets = held.tile([P, N // 16], U16, name="offsets")
         nc.sync.dma_start(offsets[:], offs)
         table_sb = held.tile([P, V], BF16, name="table_sb")
-        nc.sync.dma_start(table_sb[:], table)
+        nc.scalar.dma_start(table_sb[:], table)
+        w_sb = held.tile([P, 2 * P], BF16, name="w_sb")
+        nc.sync.dma_start(w_sb[:], w)
         cos_sb = held.tile([P, N], F32, name="cos_sb")
         nc.sync.dma_start(cos_sb[:], cosr)
         sin_sb = held.tile([P, N], F32, name="sin_sb")
-        nc.sync.dma_start(sin_sb[:], sinr)
-        w_sb = held.tile([P, 2 * P], BF16, name="w_sb")
-        nc.scalar.dma_start(w_sb[:], w)
-        b_qk = held.tile([P, 1], F32, name="b_qk")
-        nc.scalar.dma_start(b_qk[:], b[0:P, :])
+        nc.scalar.dma_start(sin_sb[:], sinr)
+
+        one = held.tile([1, 1], F32, name="one")
+        nc.vector.memset(one[:], 1.0)
+        warm = held.tile([1, 1], F32, name="warm")
+        nc.scalar.activation(warm[:], one[:], IDENTITY)
 
         w_rot = held.tile([P, P], BF16, name="w_rot")
-        b_rot = held.tile([P, 1], F32, name="b_rot")
-        for low in range(0, P, HEAD):
-            high = low + HALF
-            nc.scalar.dma_start(b_rot[low : low + HALF, :], b[high : high + HALF, :])
-            nc.scalar.dma_start(b_rot[high : high + HALF, :], b[low : low + HALF, :])
-            nc.vector.tensor_scalar_mul(b_rot[low : low + HALF, :], b_rot[low : low + HALF, :], -1.0)
-            nc.vector.tensor_scalar_mul(w_rot[:, low : low + HALF], w_sb[:, high : high + HALF], -1.0)
-            nc.vector.tensor_copy(w_rot[:, high : high + HALF], w_sb[:, low : low + HALF])
+        b_rot_row = held.tile([1, P], F32, name="b_rot_row")
+        for rotated, plain in ((b_rot_row[:], b_row[:, 0:P]), (w_rot[:], w_sb[:, 0:P])):
+            halves_out = rotated.rearrange("p (head half k) -> p head half k", half=2, k=HALF)
+            halves_in = plain.rearrange("p (head half k) -> p head half k", half=2, k=HALF)
+            nc.vector.tensor_scalar_mul(halves_out[:, :, 0, :], halves_in[:, :, 1, :], -1.0)
+            nc.vector.tensor_copy(halves_out[:, :, 1, :], halves_in[:, :, 0, :])
 
-        b_val = held.tile([P, 1], F32, name="b_val")
-        nc.scalar.dma_start(b_val[:], b[P : 2 * P, :])
+        bias_ps = banks.tile([P, 3], F32, name="bias_ps")
+        nc.tensor.matmul(bias_ps[:, 0:1], b_row[:, 0:P], one[:], start=True, stop=True)
+        nc.tensor.matmul(bias_ps[:, 1:2], b_rot_row[:], one[:], start=True, stop=True)
+        nc.tensor.matmul(bias_ps[:, 2:3], b_row[:, P : 2 * P], one[:], start=True, stop=True)
+        bias = held.tile([P, 3], F32, name="bias")
+        nc.vector.tensor_copy(bias[:], bias_ps[:])
+        b_qk, b_rot, b_val = bias[:, 0:1], bias[:, 1:2], bias[:, 2:3]
 
         picked = table_sb[:].indirect(offsets[:])
         p_qk = banks.tile([P, N], F32, name="p_qk")
@@ -50,13 +57,13 @@ def tile_kelso_model_kernel(tc, table, w, b, cosr, sinr, offs, out):
         nc.tensor.matmul(p_val[:], w_sb[:, P : 2 * P], picked, start=True, stop=True)
 
         with_cos = held.tile([P, N], F32, name="with_cos")
-        nc.vector.scalar_tensor_tensor(with_cos[:], p_qk[:], b_qk[:], cos_sb[:], op0=ADD, op1=MULT)
+        nc.vector.scalar_tensor_tensor(with_cos[:], p_qk[:], b_qk, cos_sb[:], op0=ADD, op1=MULT)
         with_sin = held.tile([P, N], F32, name="with_sin")
-        nc.vector.scalar_tensor_tensor(with_sin[:], r_qk[:], b_rot[:], sin_sb[:], op0=ADD, op1=MULT)
+        nc.vector.scalar_tensor_tensor(with_sin[:], r_qk[:], b_rot, sin_sb[:], op0=ADD, op1=MULT)
         out_qk = held.tile([P, N], F32, name="out_qk")
         nc.vector.tensor_add(out_qk[:], with_cos[:], with_sin[:])
         nc.sync.dma_start(out[0:P, :], out_qk[:])
 
         out_val = held.tile([P, N], F32, name="out_val")
-        nc.scalar.activation(out_val[:], p_val[:], IDENTITY, bias=b_val[:])
+        nc.scalar.activation(out_val[:], p_val[:], IDENTITY, bias=b_val)
         nc.scalar.dma_start(out[P : 2 * P, :], out_val[:])

@@ -4,6 +4,8 @@ P = 128
 V = 1024
 N = 256
 HALF = 32
+PIECES = 2
+PIECE = N // PIECES
 FLOPS = 2 * P * 2 * P * N
 
 BF16, F32, U16 = mybir.dt.bfloat16, mybir.dt.float32, mybir.dt.uint16
@@ -49,21 +51,24 @@ def tile_kelso_model_kernel(tc, table, w, b, cosr, sinr, offs, out):
         b_qk, b_rot, b_val = bias[:, 0:1], bias[:, 1:2], bias[:, 2:3]
 
         picked = table_sb[:].indirect(offsets[:])
-        p_qk = banks.tile([P, N], F32, name="p_qk")
-        nc.tensor.matmul(p_qk[:], w_sb[:, 0:P], picked, start=True, stop=True)
-        r_qk = banks.tile([P, N], F32, name="r_qk")
-        nc.tensor.matmul(r_qk[:], w_rot[:], picked, start=True, stop=True)
         p_val = banks.tile([P, N], F32, name="p_val")
         nc.tensor.matmul(p_val[:], w_sb[:, P : 2 * P], picked, start=True, stop=True)
-
-        with_cos = held.tile([P, N], F32, name="with_cos")
-        nc.vector.scalar_tensor_tensor(with_cos[:], p_qk[:], b_qk, cos_sb[:], op0=ADD, op1=MULT)
-        with_sin = held.tile([P, N], F32, name="with_sin")
-        nc.vector.scalar_tensor_tensor(with_sin[:], r_qk[:], b_rot, sin_sb[:], op0=ADD, op1=MULT)
-        out_qk = held.tile([P, N], F32, name="out_qk")
-        nc.vector.tensor_add(out_qk[:], with_cos[:], with_sin[:])
-        nc.sync.dma_start(out[0:P, :], out_qk[:])
-
         out_val = held.tile([P, N], F32, name="out_val")
         nc.scalar.activation(out_val[:], p_val[:], IDENTITY, bias=b_val)
         nc.scalar.dma_start(out[P : 2 * P, :], out_val[:])
+
+        p_qk = banks.tile([P, N], F32, name="p_qk")
+        nc.tensor.matmul(p_qk[:], w_sb[:, 0:P], picked, start=True, stop=True)
+        with_cos = held.tile([P, N], F32, name="with_cos")
+        nc.vector.scalar_tensor_tensor(with_cos[:], p_qk[:], b_qk, cos_sb[:], op0=ADD, op1=MULT)
+
+        with_sin = held.tile([P, N], F32, name="with_sin")
+        out_qk = held.tile([P, N], F32, name="out_qk")
+        for piece in range(PIECES):
+            cols = slice(piece * PIECE, (piece + 1) * PIECE)
+            picked_piece = table_sb[:].indirect(offsets[:, piece * (PIECE // 16) : (piece + 1) * (PIECE // 16)])
+            r_qk = banks.tile([P, PIECE], F32, name="r_qk%d" % piece)
+            nc.tensor.matmul(r_qk[:], w_rot[:], picked_piece, start=True, stop=True)
+            nc.vector.scalar_tensor_tensor(with_sin[:, cols], r_qk[:], b_rot, sin_sb[:, cols], op0=ADD, op1=MULT)
+            nc.vector.tensor_add(out_qk[:, cols], with_cos[:, cols], with_sin[:, cols])
+        nc.sync.dma_start(out[0:P, :], out_qk[:])

@@ -16,14 +16,22 @@ IDENTITY = mybir.ActivationFunctionType.Identity
 def tile_kelso_model_kernel(tc, table, w, b, cosr, sinr, offs, out):
     nc = tc.nc
     with tc.tile_pool(name="held", bufs=1) as held, tc.psum_pool(name="banks", bufs=1) as banks:
-        b_row = held.tile([1, 2 * P], F32, name="b_row")
-        nc.scalar.dma_start(b_row[:], b.rearrange("m one -> one m"))
+        b_rows = held.tile([P, 4 * HALF], F32, name="b_rows", align_bytes=64)
+        nc.vector.memset(b_rows[:], 0.0)
+
         offsets = held.tile([P, N // 16], U16, name="offsets")
         nc.sync.dma_start(offsets[:], offs)
         table_sb = held.tile([P, V], BF16, name="table_sb")
         nc.scalar.dma_start(table_sb[:], table)
         w_sb = held.tile([P, 2 * P], BF16, name="w_sb")
         nc.sync.dma_start(w_sb[:], w)
+        nc.sync.dma_start(
+            b_rows[0:P:HALF, 0 : 2 * HALF].rearrange("group (a k) -> group a k", a=2),
+            b.rearrange("(a group k) one -> group a (k one)", a=2, k=HALF),
+        )
+        b_halves = b[0:P, :].rearrange("(head half k) one -> half head (k one)", half=2, k=HALF)
+        for half in range(2):
+            nc.scalar.dma_start(b_rows[half * HALF : P : 2 * HALF, 2 * HALF : 3 * HALF], b_halves[1 - half])
         cos_sb = held.tile([P, N], F32, name="cos_sb")
         nc.sync.dma_start(cos_sb[:], cosr)
         sin_sb = held.tile([P, N], F32, name="sin_sb")
@@ -35,20 +43,18 @@ def tile_kelso_model_kernel(tc, table, w, b, cosr, sinr, offs, out):
         nc.scalar.activation(warm[:], one[:], IDENTITY)
 
         w_rot = held.tile([P, P], BF16, name="w_rot")
-        b_rot_row = held.tile([1, P], F32, name="b_rot_row")
-        for rotated, plain in ((b_rot_row[:], b_row[:, 0:P]), (w_rot[:], w_sb[:, 0:P])):
-            halves_out = rotated.rearrange("p (head half k) -> p head half k", half=2, k=HALF)
-            halves_in = plain.rearrange("p (head half k) -> p head half k", half=2, k=HALF)
-            nc.vector.tensor_scalar_mul(halves_out[:, :, 0, :], halves_in[:, :, 1, :], -1.0)
-            nc.vector.tensor_copy(halves_out[:, :, 1, :], halves_in[:, :, 0, :])
+        halves_out = w_rot[:].rearrange("p (head half k) -> p head half k", half=2, k=HALF)
+        halves_in = w_sb[:, 0:P].rearrange("p (head half k) -> p head half k", half=2, k=HALF)
+        nc.vector.tensor_copy(halves_out, halves_in[:, :, ::-1, :])
 
-        bias_ps = banks.tile([P, 3], F32, name="bias_ps")
-        nc.tensor.matmul(bias_ps[:, 0:1], b_row[:, 0:P], one[:], start=True, stop=True)
-        nc.tensor.matmul(bias_ps[:, 1:2], b_rot_row[:], one[:], start=True, stop=True)
-        nc.tensor.matmul(bias_ps[:, 2:3], b_row[:, P : 2 * P], one[:], start=True, stop=True)
-        bias = held.tile([P, 3], F32, name="bias")
-        nc.vector.tensor_copy(bias[:], bias_ps[:])
-        b_qk, b_rot, b_val = bias[:, 0:1], bias[:, 1:2], bias[:, 2:3]
+        sign = held.tile([P, 1], F32, name="sign")
+        nc.vector.memset(sign[:], 1.0)
+        for head in range(P // (2 * HALF)):
+            nc.vector.memset(sign[2 * HALF * head : 2 * HALF * head + HALF, :], -1.0)
+
+        b_cols = held.tile([P, 4 * HALF], F32, name="b_cols", align_bytes=64)
+        nc.vector.transpose(b_cols[:], b_rows[:])
+        b_qk, b_val, b_rot = (b_cols[:, block * HALF : block * HALF + 1] for block in range(3))
 
         picked = table_sb[:].indirect(offsets[:])
         p_val = banks.tile([P, N], F32, name="p_val")
@@ -67,8 +73,10 @@ def tile_kelso_model_kernel(tc, table, w, b, cosr, sinr, offs, out):
         for piece in range(PIECES):
             cols = slice(piece * PIECE, (piece + 1) * PIECE)
             picked_piece = table_sb[:].indirect(offsets[:, piece * (PIECE // 16) : (piece + 1) * (PIECE // 16)])
-            r_qk = banks.tile([P, PIECE], F32, name="r_qk%d" % piece)
-            nc.tensor.matmul(r_qk[:], w_rot[:], picked_piece, start=True, stop=True)
-            nc.vector.scalar_tensor_tensor(with_sin[:, cols], r_qk[:], b_rot, sin_sb[:, cols], op0=ADD, op1=MULT)
-            nc.vector.tensor_add(out_qk[:, cols], with_cos[:, cols], with_sin[:, cols])
+            q_qk = banks.tile([P, PIECE], F32, name="q_qk%d" % piece)
+            nc.tensor.matmul(q_qk[:], w_rot[:], picked_piece, start=True, stop=True)
+            nc.vector.scalar_tensor_tensor(with_sin[:, cols], q_qk[:], b_rot, sin_sb[:, cols], op0=ADD, op1=MULT)
+            nc.vector.scalar_tensor_tensor(
+                out_qk[:, cols], with_sin[:, cols], sign[:], with_cos[:, cols], op0=MULT, op1=ADD
+            )
         nc.sync.dma_start(out[0:P, :], out_qk[:])

import concourse.mybir as mybir

P = 128
V = 1024
N = 256
HALF = 32
PIECES = 2
PIECE = N // PIECES
FLOPS = 2 * P * 2 * P * N

BF16, F32, U16 = mybir.dt.bfloat16, mybir.dt.float32, mybir.dt.uint16
ADD, MULT = mybir.AluOpType.add, mybir.AluOpType.mult
IDENTITY = mybir.ActivationFunctionType.Identity


def tile_kelso_model_kernel(tc, table, w, b, cosr, sinr, offs, out):
    nc = tc.nc
    with tc.tile_pool(name="held", bufs=1) as held, tc.psum_pool(name="banks", bufs=1) as banks:
        b_rows = held.tile([P, 4 * HALF], F32, name="b_rows", align_bytes=64)
        nc.vector.memset(b_rows[:], 0.0)

        offsets = held.tile([P, N // 16], U16, name="offsets")
        nc.sync.dma_start(offsets[:], offs)
        table_sb = held.tile([P, V], BF16, name="table_sb")
        nc.scalar.dma_start(table_sb[:], table)
        w_sb = held.tile([P, 2 * P], BF16, name="w_sb")
        nc.sync.dma_start(w_sb[:], w)
        nc.sync.dma_start(
            b_rows[0:P:HALF, 0 : 2 * HALF].rearrange("group (a k) -> group a k", a=2),
            b.rearrange("(a group k) one -> group a (k one)", a=2, k=HALF),
        )
        b_halves = b[0:P, :].rearrange("(head half k) one -> half head (k one)", half=2, k=HALF)
        for half in range(2):
            nc.scalar.dma_start(b_rows[half * HALF : P : 2 * HALF, 2 * HALF : 3 * HALF], b_halves[1 - half])
        cos_sb = held.tile([P, N], F32, name="cos_sb")
        nc.sync.dma_start(cos_sb[:], cosr)
        sin_sb = held.tile([P, N], F32, name="sin_sb")
        nc.scalar.dma_start(sin_sb[:], sinr)

        one = held.tile([1, 1], F32, name="one")
        nc.vector.memset(one[:], 1.0)
        warm = held.tile([1, 1], F32, name="warm")
        nc.scalar.activation(warm[:], one[:], IDENTITY)

        w_rot = held.tile([P, P], BF16, name="w_rot")
        halves_out = w_rot[:].rearrange("p (head half k) -> p head half k", half=2, k=HALF)
        halves_in = w_sb[:, 0:P].rearrange("p (head half k) -> p head half k", half=2, k=HALF)
        nc.vector.tensor_copy(halves_out, halves_in[:, :, ::-1, :])

        sign = held.tile([P, 1], F32, name="sign")
        nc.vector.memset(sign[:], 1.0)
        for head in range(P // (2 * HALF)):
            nc.vector.memset(sign[2 * HALF * head : 2 * HALF * head + HALF, :], -1.0)

        b_cols = held.tile([P, 4 * HALF], F32, name="b_cols", align_bytes=64)
        nc.vector.transpose(b_cols[:], b_rows[:])
        b_qk, b_val, b_rot = (b_cols[:, block * HALF : block * HALF + 1] for block in range(3))

        picked = table_sb[:].indirect(offsets[:])
        p_val = banks.tile([P, N], F32, name="p_val")
        nc.tensor.matmul(p_val[:], w_sb[:, P : 2 * P], picked, start=True, stop=True)
        out_val = held.tile([P, N], F32, name="out_val")
        nc.scalar.activation(out_val[:], p_val[:], IDENTITY, bias=b_val)
        nc.scalar.dma_start(out[P : 2 * P, :], out_val[:])

        p_qk = banks.tile([P, N], F32, name="p_qk")
        nc.tensor.matmul(p_qk[:], w_sb[:, 0:P], picked, start=True, stop=True)
        with_cos = held.tile([P, N], F32, name="with_cos")
        nc.vector.scalar_tensor_tensor(with_cos[:], p_qk[:], b_qk, cos_sb[:], op0=ADD, op1=MULT)

        with_sin = held.tile([P, N], F32, name="with_sin")
        out_qk = held.tile([P, N], F32, name="out_qk")
        for piece in range(PIECES):
            cols = slice(piece * PIECE, (piece + 1) * PIECE)
            picked_piece = table_sb[:].indirect(offsets[:, piece * (PIECE // 16) : (piece + 1) * (PIECE // 16)])
            q_qk = banks.tile([P, PIECE], F32, name="q_qk%d" % piece)
            nc.tensor.matmul(q_qk[:], w_rot[:], picked_piece, start=True, stop=True)
            nc.vector.scalar_tensor_tensor(with_sin[:, cols], q_qk[:], b_rot, sin_sb[:, cols], op0=ADD, op1=MULT)
            nc.vector.scalar_tensor_tensor(
                out_qk[:, cols], with_sin[:, cols], sign[:], with_cos[:, cols], op0=MULT, op1=ADD
            )
        nc.sync.dma_start(out[0:P, :], out_qk[:])
